import numpy as np
import ml_dtypes


def mxq(x, axis, fmt="e4m3"):
    dtype, down = {"e4m3": (ml_dtypes.float8_e4m3fn, 7), "e5m2": (ml_dtypes.float8_e5m2, 14)}[fmt]
    v = np.moveaxis(np.asarray(x, np.float32).astype(ml_dtypes.bfloat16).astype(np.float64), axis, -1)
    blocks = v.reshape(v.shape[:-1] + (-1, 32))
    amax = np.abs(blocks).max(-1, keepdims=True)
    byte = np.maximum(np.where(amax > 0, np.frexp(amax)[1] - 1 + 127, 0) - down, 1)
    scale = np.exp2(byte - 127.0)
    codes = (blocks / scale).astype(np.float32).astype(dtype).astype(np.float64)
    return np.moveaxis((codes * scale).reshape(v.shape), -1, axis)


WIDE = False


def mx_kscale(k):
    if not WIDE:
        return np.ones(k)
    levels = np.array([10, -10, 5, -5, 0])
    if k % 512:
        return np.exp2(np.random.permutation(np.resize(levels, k // 32))).repeat(32)
    a = np.empty((k // 512, 16))
    for p in range(k // 512):
        a[p, :8] = np.random.permutation(np.resize(levels, 8))
        for g in range(8):
            far = levels[np.abs(levels - a[p, g]) >= 10]
            a[p, g + 8] = far[np.random.randint(len(far))]
    return np.exp2(a.ravel()).repeat(32)


BF16 = ml_dtypes.bfloat16


def bf(x):
    return np.asarray(x, np.float32).astype(BF16)


def f64(x):
    return np.asarray(x).astype(np.float64)


E2M1 = np.array([0.0, 0.5, 1.0, 1.5, 2.0, 3.0, 4.0, 6.0, -0.0, -0.5, -1.0, -1.5, -2.0, -3.0, -4.0, -6.0])


def pack_weight(w, fmt):
    k, n = w.shape
    w = f64(bf(w)).reshape(k // 32, 32, n)
    amax = np.abs(w).max(1)
    if fmt == "e4m3":
        byte = np.frexp(amax)[1] - 1 + 127 - 7
    else:
        mant, ex = np.frexp(amax / 6.0)
        byte = np.where(mant > 0.5, ex, ex - 1) + 127
    byte = np.clip(np.where(amax > 0, byte, 1), 1, 254)
    scaled = (w * np.exp2(127.0 - byte)[:, None, :]).reshape(k, n).astype(np.float32)
    by_word = np.ascontiguousarray(scaled.reshape(k // 512, 128, 4, n).transpose(0, 1, 3, 2))
    if fmt == "e4m3":
        words = by_word.astype(ml_dtypes.float8_e4m3fn).view(np.uint8)
    else:
        c = by_word.astype(ml_dtypes.float4_e2m1fn).view(np.uint8) & 0xF
        words = c[..., 0::2] | (c[..., 1::2] << 4)
    return np.ascontiguousarray(words), np.ascontiguousarray(byte.astype(np.uint8).reshape(k // 512, 16, n))


def unpack_weight(words, scales, fmt):
    g, p, n, _ = words.shape
    if fmt == "e4m3":
        vals = np.ascontiguousarray(words).view(ml_dtypes.float8_e4m3fn).astype(np.float64)
    else:
        nib = np.empty((g, p, n, 4), np.uint8)
        nib[..., 0::2] = words & 0xF
        nib[..., 1::2] = words >> 4
        vals = E2M1[nib]
    vals = vals * np.repeat(np.exp2(scales.astype(np.float64) - 127.0), 8, axis=1)[..., None]
    return vals.transpose(0, 1, 3, 2).reshape(g * 512, n)


B, S, D_MODEL, N_HEADS, D_KV, D_ROPE = 4, 2048, 512, 8, 512, 16
D_HEAD = D_MODEL // N_HEADS
SPLIT = D_HEAD - D_ROPE
ROT_SCALE = 40.0
ROT_BASE = 10000.0


def rotate_half(x):
    x1, x2 = np.split(x, 2, axis=-1)
    return np.concatenate((-x2, x1), axis=-1)


def apply_rotary(x, cos, sin):
    r = cos.shape[-1]
    x_rot, x_base = x[..., :r], x[..., r:]
    x_rot = x_rot * cos + rotate_half(x_rot) * sin
    return np.concatenate((x_rot, x_base), axis=-1)


def rotary_emb(seq_len):
    exps = np.arange(0, D_ROPE // 2, 2, dtype=np.float64) / (D_ROPE // 2)
    inv_freq = 1.0 / ROT_BASE ** exps
    t = np.arange(seq_len, dtype=np.float64) / ROT_SCALE
    freqs = t[:, None] * inv_freq[None, :]
    return np.concatenate((freqs, freqs), axis=-1)


def draw0():
    s, t = mx_kscale(D_MODEL), mx_kscale(D_KV)
    h = bf(np.random.standard_normal((B, S, D_MODEL)) * s)
    W_dq_words, W_dq_scales = pack_weight(np.random.standard_normal((D_MODEL, D_KV)) / np.sqrt(D_MODEL) / s[:, None] * t, "e4m3")
    b_dq = bf(np.random.standard_normal(D_KV) * 0.3 * t)
    W_uq_words, W_uq_scales = pack_weight(np.random.standard_normal((D_KV, N_HEADS * SPLIT)) / np.sqrt(D_KV) / t[:, None], "e4m3")
    b_uq = bf(np.random.standard_normal(N_HEADS * SPLIT) * 0.3)
    W_qr_words, W_qr_scales = pack_weight(np.random.standard_normal((D_KV, N_HEADS * D_ROPE)) * 2.0 / np.sqrt(D_KV) / t[:, None], "e4m3")
    b_qr = bf(np.random.standard_normal(N_HEADS * D_ROPE) * 0.5)
    return {
        "h": h,
        "W_dq_words": W_dq_words,
        "W_dq_scales": W_dq_scales,
        "b_dq": b_dq,
        "W_uq_words": W_uq_words,
        "W_uq_scales": W_uq_scales,
        "b_uq": b_uq,
        "W_qr_words": W_qr_words,
        "W_qr_scales": W_qr_scales,
        "b_qr": b_qr,
    }


def core(h, W_dq_words, W_dq_scales, b_dq, W_uq_words, W_uq_scales, b_uq, W_qr_words, W_qr_scales, b_qr):
    c_q = (mxq(f64(h), 2, "e4m3") @ unpack_weight(W_dq_words, W_dq_scales, "e4m3")) + f64(b_dq)
    cq = mxq(c_q, 2, "e4m3")
    q_base = ((cq @ unpack_weight(W_uq_words, W_uq_scales, "e4m3")) + f64(b_uq)).reshape(B, S, N_HEADS, SPLIT)
    q_rot = ((cq @ unpack_weight(W_qr_words, W_qr_scales, "e4m3")) + f64(b_qr)).reshape(B, S, N_HEADS, D_ROPE)
    emb = rotary_emb(S)
    cos = np.cos(emb).reshape(1, S, 1, -1)
    sin = np.sin(emb).reshape(1, S, 1, -1)
    q_rot = apply_rotary(q_rot, cos, sin)
    return np.concatenate((q_base, q_rot), axis=-1)


def e4m3fn_bytes(y):
    return np.clip(np.asarray(y, np.float64), -448.0, 448.0).astype(np.float32).astype(ml_dtypes.float8_e4m3fn).view(np.uint8)


def e4m3fn_values(b):
    return np.asarray(b, np.uint8).view(ml_dtypes.float8_e4m3fn).astype(np.float64)


def setup_inputs():
    d = draw0()
    x0 = np.asarray(d['h']).astype(np.float64)
    s = (np.max(np.abs(x0), axis=(0, 1), keepdims=True) / 448.0).astype(np.float32)
    out = {}
    for k, v in d.items():
        if k == 'h':
            out['h_bytes'] = e4m3fn_bytes(x0 / s.astype(np.float64))
            out['h_scale'] = s
        else:
            out[k] = v
    return out


def reference(h_bytes, h_scale, W_dq_words, W_dq_scales, b_dq, W_uq_words, W_uq_scales, b_uq, W_qr_words, W_qr_scales, b_qr):
    return core(e4m3fn_values(h_bytes) * h_scale.astype(np.float64), W_dq_words, W_dq_scales, b_dq, W_uq_words, W_uq_scales, b_uq, W_qr_words, W_qr_scales, b_qr)

@@ -1,0 +1,291 @@
+from contextlib import ExitStack
+import math
+
+import concourse.mybir as mybir
+from concourse.masks import make_identity
+
+B, S, D, HEADS = 4, 2048, 512, 8
+TOKENS = B * S
+FLOPS = 2 * TOKENS * D * (D + 384 + 128)
+
+F32 = mybir.dt.float32
+BF16 = mybir.dt.bfloat16
+I32 = mybir.dt.int32
+U8 = mybir.dt.uint8
+F8 = mybir.dt.float8_e4m3fn
+X4 = mybir.dt.float8_e4m3fn_x4
+ACT = mybir.ActivationFunctionType
+ALU = mybir.AluOpType
+
+P = 128
+J = 4
+GROUP = P * J
+GROUPS = TOKENS // GROUP
+
+
+def tile_mla_pa_t_w8_kernel(tc, h_bytes, h_scale, wdq_w, wdq_s, b_dq, wuq_w, wuq_s, b_uq, wqr_w, wqr_s, b_qr, out):
+    nc = tc.nc
+    h_view = h_bytes.rearrange("b s k -> (b s) k").rearrange("(m p j) k -> m p (j k)", p=P, j=J)
+    out_view = out.rearrange("b s h d -> (b s) (h d)").rearrange("(m p j) f -> m p (j f)", p=P, j=J)
+
+    with ExitStack() as ctx:
+        const = ctx.enter_context(tc.tile_pool(name="const", bufs=1))
+        work = ctx.enter_context(tc.tile_pool(name="work", bufs=2))
+        psum = ctx.enter_context(tc.psum_pool(name="psum", bufs=8))
+        ctx.enter_context(tc.manual_schedule())
+
+        hb = [const.tile([P, J * D], U8, name="hb%d" % m, align_bytes=64) for m in range(GROUPS)]
+        wraw = const.tile([P, 1024], I32, name="wraw", align_bytes=64)
+        sraw = const.tile([P, 1024], U8, name="sraw", align_bytes=64)
+        wdq = const.tile([P, 4, P], I32, name="wdq", align_bytes=64)
+        sdq = const.tile([P, 4, P], U8, name="sdq", align_bytes=64)
+        wout = const.tile([P, 512], I32, name="wout", align_bytes=64)
+        sout = const.tile([P, 512], U8, name="sout", align_bytes=64)
+        s4 = const.tile([P, 4], F32, name="s4")
+        bdq_bf = const.tile([P, 4], BF16, name="bdq_bf")
+        bdq = const.tile([P, 4], F32, name="bdq")
+        bbc = const.tile([P, 512], BF16, name="bbc")
+        bias_t = const.tile([P, 512], F32, name="bias_t")
+        bcol = const.tile([P, 2], F32, name="bcol")
+        ident = const.tile([P, P], F32, name="ident")
+        ang = const.tile([P, 16, 4], F32, name="ang")
+        gem = const.tile([P, 16, 4], F32, name="gem")
+        posn = const.tile([P, 16], F32, name="posn")
+        sinw = const.tile([P, 16, 4], F32, name="sinw")
+        sinv = const.tile([P, 16, 4], F32, name="sinv")
+        c8 = const.tile([P, 16, 8], F32, name="c8")
+        s8 = const.tile([P, 16, 8], F32, name="s8")
+        dummy = const.tile([P, 1], F32, name="dummy")
+        dummy2 = const.tile([P, 1], F32, name="dummy2")
+
+        sraw32 = sraw[:].bitcast(I32)
+
+        def load_scales(src, first, width):
+            for q in range(4):
+                nc.sync.dma_start(
+                    out=sraw32[32 * q : 32 * q + 4, first // 4 : (first + width) // 4],
+                    in_=src[0][4 * q : 4 * q + 4, :].bitcast(I32),
+                )
+
+        nc.vector.memset(sraw32, 0)
+        nc.vector.memset(dummy[:], 0.0)
+        nc.scalar.activation(out=dummy2[:], in_=dummy[:], func=ACT.Sin)
+        make_identity(nc, ident[:])
+
+        nc.sync.dma_start(out=hb[0][:], in_=h_view[0])
+        nc.sync.dma_start(out=wraw[:, 0:512], in_=wdq_w[0].rearrange("p n t -> p (n t)").bitcast(I32))
+        nc.sync.dma_start(out=s4[:], in_=h_scale.rearrange("o a (p t) -> p (o a t)", t=4))
+        load_scales(wdq_s, 0, 512)
+        nc.sync.dma_start(out=bdq_bf[:], in_=b_dq.rearrange("(p t) -> p t", t=4))
+        nc.sync.dma_start(out=hb[1][:], in_=h_view[1])
+        nc.sync.dma_start(out=wraw[:, 512:896], in_=wuq_w[0].rearrange("p n t -> p (n t)").bitcast(I32))
+        nc.sync.dma_start(out=wraw[:, 896:1024], in_=wqr_w[0].rearrange("p n t -> p (n t)").bitcast(I32))
+        load_scales(wuq_s, 512, 384)
+        load_scales(wqr_s, 896, 128)
+        nc.sync.dma_start(out=hb[2][:], in_=h_view[2])
+        nc.sync.dma_start(out=bbc[:, 0:384], in_=b_uq.partition_broadcast(P))
+        nc.sync.dma_start(out=bbc[:, 384:512], in_=b_qr.partition_broadcast(P))
+        for m in range(3, GROUPS):
+            nc.sync.dma_start(out=hb[m][:], in_=h_view[m])
+
+        nc.vector.tensor_copy(out=wdq[:], in_=wraw[:, 0:512].rearrange("p (m t) -> p t m", t=4))
+        nc.gpsimd.tensor_copy(out=sdq[:].rearrange("p t m -> p m t"), in_=sraw[:, 0:512].rearrange("p (m t) -> p m t", t=4))
+        nc.gpsimd.tensor_copy(out=bdq[:], in_=bdq_bf[:])
+
+        def regroup(dst, src):
+            uq = src[:, 0:384].rearrange("p (h c) -> p h c", c=48)
+            qr = src[:, 384:512].rearrange("p (h c) -> p h c", c=16)
+            rest = dst[:, 256:512].rearrange("p (h c) -> p h c", c=32)
+            for x in range(2):
+                nc.gpsimd.tensor_copy(
+                    out=dst[:, P * x : P * (x + 1)].rearrange("p (h c) -> p h c", c=16), in_=uq[:, :, 16 * x : 16 * (x + 1)]
+                )
+            nc.gpsimd.tensor_copy(out=rest[:, :, 0:16], in_=uq[:, :, 32:48])
+            nc.gpsimd.tensor_copy(out=rest[:, :, 16:32], in_=qr)
+
+        regroup(wout, wraw[:, 512:1024])
+        regroup(sout, sraw[:, 512:1024])
+        regroup(bias_t, bbc)
+
+        nc.gpsimd.iota(posn[:].rearrange("p (q j) -> p q j", j=4), pattern=[[512, 4], [1, 4]], base=0, channel_multiplier=4, allow_small_or_imprecise_dtypes=True)
+        for i in range(4):
+            nc.gpsimd.tensor_scalar(out=ang[:, :, i], in0=posn[:], scalar1=1.0 / (80.0 * math.pi * 10.0**i), scalar2=None, op0=ALU.mult)
+        for turns in (8.0, 4.0, 2.0, 1.0):
+            nc.gpsimd.tensor_scalar(out=gem[:], in0=ang[:], scalar1=turns, scalar2=-turns, op0=ALU.is_ge, op1=ALU.mult)
+            nc.gpsimd.tensor_tensor(out=ang[:], in0=ang[:], in1=gem[:], op=ALU.add)
+        nc.gpsimd.tensor_scalar(out=ang[:], in0=ang[:], scalar1=1.0, scalar2=-0.5, op0=ALU.mult, op1=ALU.add)
+
+        def rotary_tables():
+            nc.scalar.activation(out=sinw[:], in_=ang[:], func=ACT.Sin, scale=2.0 * math.pi)
+            nc.scalar.activation(out=sinv[:], in_=ang[:], func=ACT.Sin, scale=math.pi)
+            nc.gpsimd.tensor_tensor(out=sinv[:], in0=sinv[:], in1=sinv[:], op=ALU.mult)
+            for half in range(2):
+                cols = slice(4 * half, 4 * half + 4)
+                nc.gpsimd.tensor_scalar(out=c8[:, :, cols], in0=sinv[:], scalar1=2.0, scalar2=-1.0, op0=ALU.mult, op1=ALU.add)
+                nc.gpsimd.tensor_scalar(out=s8[:, :, cols], in0=sinw[:], scalar1=1.0 - 2.0 * half, scalar2=0.0, op0=ALU.mult, op1=ALU.add)
+
+        def bias_columns():
+            bank = psum.tile([P, 512], F32, name="bank")
+            for x in range(2):
+                nc.tensor.transpose(bank[:, P * x : P * (x + 1)], bias_t[:, P * x : P * (x + 1)], ident[:])
+            nc.vector.tensor_copy(out=bcol[:], in_=bank[:, 0:256].rearrange("p (x r) -> p x r", x=2)[:, :, 0])
+
+        st = [{} for m in range(GROUPS)]
+
+        def widen(m, b):
+            s = st[m]
+            if b == 0:
+                wide = work.tile([P, J * D], BF16, name="wide", align_bytes=64)
+                s["wide"] = wide
+            cols = slice(1024 * b, 1024 * (b + 1))
+            nc.scalar.copy(out=s["wide"][:, cols], in_=hb[m][:, cols].bitcast(F8))
+
+        def turn(m, b):
+            bank = psum.tile([P, 512], F32, name="bank")
+            view = bank[:].rearrange("p (u r) -> p u r", u=2)
+            words = st[m]["wide"][:].bitcast(F32)
+            for jj in range(2):
+                for u in range(2):
+                    base = 256 * (2 * b + jj)
+                    nc.tensor.transpose(view[:, u, P * jj : P * (jj + 1)], words[:, base + u : base + 256 : 2], ident[:])
+            st[m]["x%d" % b] = bank
+
+        def scale(m, b):
+            s = st[m]
+            if b == 0:
+                grp = work.tile([P, J * D], BF16, name="grp", align_bytes=64)
+                s["grp"] = grp
+            nc.vector.tensor_tensor(
+                out=s["grp"][:, 1024 * b : 1024 * (b + 1)].rearrange("p (r u e) -> p r u e", u=2, e=2),
+                in0=s["x%d" % b][:].bitcast(BF16).rearrange("p (u r e) -> p r u e", u=2, e=2),
+                in1=s4[:].rearrange("p (u e) -> p u e", u=2).unsqueeze(1).to_broadcast([P, 256, 2, 2]),
+                op=ALU.mult,
+            )
+
+        def quantize(m, src, tag):
+            codes = work.tile([P, 512], I32, name="codes" + tag, align_bytes=64)
+            scales = work.tile([P, 512], U8, name="scales" + tag, align_bytes=64)
+            nc.vector.quantize_mx(out=codes[:].bitcast(X4), scales=scales[:], in_=st[m][src][:])
+            st[m]["c" + tag] = codes
+            st[m]["s" + tag] = scales
+
+        def latent(m, t):
+            s = st[m]
+            bank = psum.tile([P, 512], F32, name="bank")
+            nc.tensor.matmul_mx(
+                out=bank[:], lhsT=wdq[:, t, :].bitcast(X4), lhsT_scale=sdq[:, t, :],
+                rhs=s["c1"][:].bitcast(X4), rhs_scale=s["s1"][:], start=True, stop=True,
+            )
+            if t == 0:
+                plane = work.tile([P, J * D], BF16, name="plane", align_bytes=64)
+                s["plane"] = plane
+            nc.scalar.activation(out=s["plane"][:, 512 * t : 512 * (t + 1)], in_=bank[:], func=ACT.Identity, bias=bdq[:, t : t + 1], scale=1.0)
+
+        def interleave(m):
+            s = st[m]
+            mixed = work.tile([P, J * D], BF16, name="mixed", align_bytes=64)
+            nc.vector.tensor_copy(
+                out=mixed[:].rearrange("p (c i t) -> p c t i", i=4, t=4), in_=s["plane"][:].rearrange("p (t c i) -> p c t i", t=4, i=4)
+            )
+            s["mixed"] = mixed
+
+        def project_rows(m, k):
+            s = st[m]
+            if k == 0:
+                rows = work.tile([P, J, 512], F32, name="rows", bufs=3)
+                s["rows"] = rows
+            bank = psum.tile([P, 512], F32, name="bank")
+            for jj in range(2):
+                toks = slice(P * (2 * k + jj), P * (2 * k + jj + 1))
+                nc.tensor.matmul_mx(
+                    out=bank[:, 256 * jj : 256 * (jj + 1)], lhsT=s["c2"][:, toks].bitcast(X4), lhsT_scale=s["s2"][:, toks],
+                    rhs=wout[:, 256:512].bitcast(X4), rhs_scale=sout[:, 256:512], start=True, stop=True,
+                )
+            nc.vector.tensor_tensor(
+                out=s["rows"][:, 2 * k : 2 * k + 2, :].rearrange("p j (h d) -> p j h d", d=64)[:, :, :, 32:64],
+                in0=bank[:].rearrange("p (j h c) -> p j h c", j=2, c=32),
+                in1=bias_t[:, 256:512].rearrange("p (h c) -> p h c", c=32).unsqueeze(1).to_broadcast([P, 2, 8, 32]),
+                op=ALU.add,
+            )
+
+        def project_columns(m, x):
+            s = st[m]
+            cols = slice(P * x, P * (x + 1))
+            bank = psum.tile([P, 512], F32, name="bank")
+            nc.tensor.matmul_mx(
+                out=bank[:], lhsT=wout[:, cols].bitcast(X4), lhsT_scale=sout[:, cols],
+                rhs=s["c2"][:].bitcast(X4), rhs_scale=s["s2"][:], start=True, stop=True,
+            )
+            cm = work.tile([P, 512], F32, name="cm%d" % x)
+            nc.scalar.activation(out=cm[:], in_=bank[:], func=ACT.Identity, bias=bcol[:, x : x + 1], scale=1.0)
+            s["cm%d" % x] = cm
+
+        def turn_back(m, x):
+            s = st[m]
+            bank = psum.tile([P, 512], F32, name="bank")
+            for j in range(J):
+                nc.tensor.transpose(bank[:, P * j : P * (j + 1)], s["cm%d" % x][:, P * j : P * (j + 1)], ident[:])
+            nc.scalar.copy(
+                out=s["rows"][:].rearrange("p j (h d) -> p j h d", d=64)[:, :, :, 16 * x : 16 * (x + 1)],
+                in_=bank[:].rearrange("p (j h c) -> p j h c", j=J, c=16),
+            )
+
+        def rotate(m):
+            x = st[m]["rows"][:].rearrange("p j (h d) -> p j h d", d=64)[:, :, :, 48:56]
+            q = 4 * (m % 4)
+            t1 = work.tile([P, J, HEADS, 8], F32, name="t1")
+            t2 = work.tile([P, J, HEADS, 8], F32, name="t2")
+            nc.gpsimd.tensor_tensor(out=t1[:], in0=x, in1=c8[:, q : q + 4, :].unsqueeze(2).to_broadcast([P, J, HEADS, 8]), op=ALU.mult)
+            for half in range(2):
+                a = slice(4 * half, 4 * half + 4)
+                b = slice(4 - 4 * half, 8 - 4 * half)
+                nc.gpsimd.tensor_tensor(
+                    out=t2[:, :, :, a], in0=x[:, :, :, b], in1=s8[:, q : q + 4, a].unsqueeze(2).to_broadcast([P, J, HEADS, 4]), op=ALU.mult
+                )
+            nc.gpsimd.tensor_tensor(out=x, in0=t1[:], in1=t2[:], op=ALU.add)
+
+        def store(m):
+            nc.sync.dma_start(out=out_view[m], in_=st[m]["rows"][:].rearrange("p j f -> p (j f)"))
+
+        def on(m):
+            return 0 <= m < GROUPS
+
+        for n in range(-1, GROUPS + 3):
+            a, b, c, d, w = n, n - 1, n - 2, n - 3, n + 1
+            if on(a):
+                turn(a, 0)
+            if on(d):
+                turn_back(d, 0)
+            if on(w):
+                widen(w, 0)
+            if on(d):
+                turn_back(d, 1)
+            if on(w):
+                widen(w, 1)
+            if n == 0:
+                rotary_tables()
+            if n == 1:
+                bias_columns()
+            if on(c):
+                interleave(c)
+            if on(a):
+                scale(a, 0)
+                turn(a, 1)
+            if on(c):
+                quantize(c, "mixed", "2")
+            if on(a):
+                scale(a, 1)
+            if on(b):
+                for t in range(4):
+                    latent(b, t)
+            if on(c):
+                project_rows(c, 0)
+                project_rows(c, 1)
+                project_columns(c, 0)
+                project_columns(c, 1)
+            if on(a):
+                quantize(a, "grp", "1")
+            if on(c):
+                rotate(c)
+            if on(d):
+                store(d)

@@ -30,7 +30,7 @@ def tile_mla_pa_t_w8_kernel(tc, h_bytes, h_scale, wdq_w, wdq_s, b_dq, wuq_w, wuq
 
     with ExitStack() as ctx:
         const = ctx.enter_context(tc.tile_pool(name="const", bufs=1))
-        work = ctx.enter_context(tc.tile_pool(name="work", bufs=2))
+        work = ctx.enter_context(tc.tile_pool(name="work", bufs=3))
         psum = ctx.enter_context(tc.psum_pool(name="psum", bufs=8))
         ctx.enter_context(tc.manual_schedule())
 
@@ -46,7 +46,7 @@ def tile_mla_pa_t_w8_kernel(tc, h_bytes, h_scale, wdq_w, wdq_s, b_dq, wuq_w, wuq
         bdq = const.tile([P, 4], F32, name="bdq")
         bbc = const.tile([P, 512], BF16, name="bbc")
         bias_t = const.tile([P, 512], F32, name="bias_t")
-        bcol = const.tile([P, 2], F32, name="bcol")
+        bcol = const.tile([P, 3], F32, name="bcol")
         ident = const.tile([P, P], F32, name="ident")
         ang = const.tile([P, 16, 4], F32, name="ang")
         gem = const.tile([P, 16, 4], F32, name="gem")
@@ -95,13 +95,11 @@ def tile_mla_pa_t_w8_kernel(tc, h_bytes, h_scale, wdq_w, wdq_s, b_dq, wuq_w, wuq
         def regroup(dst, src):
             uq = src[:, 0:384].rearrange("p (h c) -> p h c", c=48)
             qr = src[:, 384:512].rearrange("p (h c) -> p h c", c=16)
-            rest = dst[:, 256:512].rearrange("p (h c) -> p h c", c=32)
-            for x in range(2):
+            for x in range(4):
                 nc.gpsimd.tensor_copy(
-                    out=dst[:, P * x : P * (x + 1)].rearrange("p (h c) -> p h c", c=16), in_=uq[:, :, 16 * x : 16 * (x + 1)]
+                    out=dst[:, P * x : P * (x + 1)].rearrange("p (h c) -> p h c", c=16),
+                    in_=uq[:, :, 16 * x : 16 * (x + 1)] if x < 3 else qr,
                 )
-            nc.gpsimd.tensor_copy(out=rest[:, :, 0:16], in_=uq[:, :, 32:48])
-            nc.gpsimd.tensor_copy(out=rest[:, :, 16:32], in_=qr)
 
         regroup(wout, wraw[:, 512:1024])
         regroup(sout, sraw[:, 512:1024])
@@ -126,9 +124,9 @@ def tile_mla_pa_t_w8_kernel(tc, h_bytes, h_scale, wdq_w, wdq_s, b_dq, wuq_w, wuq
 
         def bias_columns():
             bank = psum.tile([P, 512], F32, name="bank")
-            for x in range(2):
+            for x in range(3):
                 nc.tensor.transpose(bank[:, P * x : P * (x + 1)], bias_t[:, P * x : P * (x + 1)], ident[:])
-            nc.vector.tensor_copy(out=bcol[:], in_=bank[:, 0:256].rearrange("p (x r) -> p x r", x=2)[:, :, 0])
+            nc.vector.tensor_copy(out=bcol[:], in_=bank[:, 0:384].rearrange("p (x r) -> p x r", x=3)[:, :, 0])
 
         st = [{} for m in range(GROUPS)]
 
@@ -169,42 +167,65 @@ def tile_mla_pa_t_w8_kernel(tc, h_bytes, h_scale, wdq_w, wdq_s, b_dq, wuq_w, wuq
             st[m]["c" + tag] = codes
             st[m]["s" + tag] = scales
 
-        def latent(m, t):
+        def latent_mm(m, out, t, toks):
+            s = st[m]
+            nc.tensor.matmul_mx(
+                out=out, lhsT=wdq[:, t, :].bitcast(X4), lhsT_scale=sdq[:, t, :],
+                rhs=s["c1"][:, toks].bitcast(X4), rhs_scale=s["s1"][:, toks], start=True, stop=True,
+            )
+
+        def latent_planes(m, half):
             s = st[m]
             bank = psum.tile([P, 512], F32, name="bank")
-            nc.tensor.matmul_mx(
-                out=bank[:], lhsT=wdq[:, t, :].bitcast(X4), lhsT_scale=sdq[:, t, :],
-                rhs=s["c1"][:].bitcast(X4), rhs_scale=s["s1"][:], start=True, stop=True,
-            )
-            if t == 0:
-                plane = work.tile([P, J * D], BF16, name="plane", align_bytes=64)
+            if half == 0:
+                plane = work.tile([P, 1024], BF16, name="plane", align_bytes=64)
                 s["plane"] = plane
-            nc.scalar.activation(out=s["plane"][:, 512 * t : 512 * (t + 1)], in_=bank[:], func=ACT.Identity, bias=bdq[:, t : t + 1], scale=1.0)
+            for i in range(2):
+                t = 2 * half + i
+                latent_mm(m, bank[:, 256 * i : 256 * (i + 1)], t, slice(256, 512))
+            for i in range(2):
+                t = 2 * half + i
+                nc.scalar.activation(
+                    out=s["plane"][:, 256 * t : 256 * (t + 1)], in_=bank[:, 256 * i : 256 * (i + 1)], func=ACT.Identity, bias=bdq[:, t : t + 1], scale=1.0
+                )
+
+        def latent_mixed(m, j):
+            s = st[m]
+            bank = psum.tile([P, 512], F32, name="bank")
+            if j == 0:
+                mixed = work.tile([P, J * D], BF16, name="mixed", align_bytes=64)
+                s["mixed"] = mixed
+            for t in range(4):
+                latent_mm(m, bank[:, P * t : P * (t + 1)], t, slice(P * j, P * (j + 1)))
+            nc.vector.tensor_tensor(
+                out=s["mixed"][:, 512 * j : 512 * (j + 1)].rearrange("p (r t) -> p r t", t=4),
+                in0=bank[:].rearrange("p (t r) -> p r t", t=4),
+                in1=bdq[:].unsqueeze(1).to_broadcast([P, P, 4]),
+                op=ALU.add,
+            )
 
         def interleave(m):
             s = st[m]
-            mixed = work.tile([P, J * D], BF16, name="mixed", align_bytes=64)
             nc.vector.tensor_copy(
-                out=mixed[:].rearrange("p (c i t) -> p c t i", i=4, t=4), in_=s["plane"][:].rearrange("p (t c i) -> p c t i", t=4, i=4)
+                out=s["mixed"][:, 1024:2048].rearrange("p (c i t) -> p c t i", i=4, t=4),
+                in_=s["plane"][:].rearrange("p (t c i) -> p c t i", t=4, i=4),
             )
-            s["mixed"] = mixed
 
-        def project_rows(m, k):
+        def project_rows(m):
             s = st[m]
-            if k == 0:
-                rows = work.tile([P, J, 512], F32, name="rows", bufs=3)
-                s["rows"] = rows
+            rows = work.tile([P, J, 512], F32, name="rows", bufs=4)
+            s["rows"] = rows
             bank = psum.tile([P, 512], F32, name="bank")
-            for jj in range(2):
-                toks = slice(P * (2 * k + jj), P * (2 * k + jj + 1))
+            for j in range(J):
+                toks = slice(P * j, P * (j + 1))
                 nc.tensor.matmul_mx(
-                    out=bank[:, 256 * jj : 256 * (jj + 1)], lhsT=s["c2"][:, toks].bitcast(X4), lhsT_scale=s["s2"][:, toks],
-                    rhs=wout[:, 256:512].bitcast(X4), rhs_scale=sout[:, 256:512], start=True, stop=True,
+                    out=bank[:, P * j : P * (j + 1)], lhsT=s["c2"][:, toks].bitcast(X4), lhsT_scale=s["s2"][:, toks],
+                    rhs=wout[:, 384:512].bitcast(X4), rhs_scale=sout[:, 384:512], start=True, stop=True,
                 )
             nc.vector.tensor_tensor(
-                out=s["rows"][:, 2 * k : 2 * k + 2, :].rearrange("p j (h d) -> p j h d", d=64)[:, :, :, 32:64],
-                in0=bank[:].rearrange("p (j h c) -> p j h c", j=2, c=32),
-                in1=bias_t[:, 256:512].rearrange("p (h c) -> p h c", c=32).unsqueeze(1).to_broadcast([P, 2, 8, 32]),
+                out=s["rows"][:].rearrange("p j (h d) -> p j h d", d=64)[:, :, :, 48:64],
+                in0=bank[:].rearrange("p (j h c) -> p j h c", j=J, c=16),
+                in1=bias_t[:, 384:512].rearrange("p (h c) -> p h c", c=16).unsqueeze(1).to_broadcast([P, J, HEADS, 16]),
                 op=ALU.add,
             )
 
@@ -230,19 +251,19 @@ def tile_mla_pa_t_w8_kernel(tc, h_bytes, h_scale, wdq_w, wdq_s, b_dq, wuq_w, wuq
                 in_=bank[:].rearrange("p (j h c) -> p j h c", j=J, c=16),
             )
 
-        def rotate(m):
+        def rotate(m, eng):
             x = st[m]["rows"][:].rearrange("p j (h d) -> p j h d", d=64)[:, :, :, 48:56]
             q = 4 * (m % 4)
             t1 = work.tile([P, J, HEADS, 8], F32, name="t1")
             t2 = work.tile([P, J, HEADS, 8], F32, name="t2")
-            nc.gpsimd.tensor_tensor(out=t1[:], in0=x, in1=c8[:, q : q + 4, :].unsqueeze(2).to_broadcast([P, J, HEADS, 8]), op=ALU.mult)
+            eng.tensor_tensor(out=t1[:], in0=x, in1=c8[:, q : q + 4, :].unsqueeze(2).to_broadcast([P, J, HEADS, 8]), op=ALU.mult)
             for half in range(2):
                 a = slice(4 * half, 4 * half + 4)
                 b = slice(4 - 4 * half, 8 - 4 * half)
-                nc.gpsimd.tensor_tensor(
+                eng.tensor_tensor(
                     out=t2[:, :, :, a], in0=x[:, :, :, b], in1=s8[:, q : q + 4, a].unsqueeze(2).to_broadcast([P, J, HEADS, 4]), op=ALU.mult
                 )
-            nc.gpsimd.tensor_tensor(out=x, in0=t1[:], in1=t2[:], op=ALU.add)
+            eng.tensor_tensor(out=x, in0=t1[:], in1=t2[:], op=ALU.add)
 
         def store(m):
             nc.sync.dma_start(out=out_view[m], in_=st[m]["rows"][:].rearrange("p j f -> p (j f)"))
@@ -254,12 +275,14 @@ def tile_mla_pa_t_w8_kernel(tc, h_bytes, h_scale, wdq_w, wdq_s, b_dq, wuq_w, wuq
             a, b, c, d, w = n, n - 1, n - 2, n - 3, n + 1
             if on(a):
                 turn(a, 0)
+                turn(a, 1)
             if on(d):
                 turn_back(d, 0)
             if on(w):
                 widen(w, 0)
             if on(d):
                 turn_back(d, 1)
+                turn_back(d, 2)
             if on(w):
                 widen(w, 1)
             if n == 0:
@@ -270,22 +293,21 @@ def tile_mla_pa_t_w8_kernel(tc, h_bytes, h_scale, wdq_w, wdq_s, b_dq, wuq_w, wuq
                 interleave(c)
             if on(a):
                 scale(a, 0)
-                turn(a, 1)
             if on(c):
                 quantize(c, "mixed", "2")
             if on(a):
                 scale(a, 1)
             if on(b):
-                for t in range(4):
-                    latent(b, t)
+                latent_planes(b, 0)
+                latent_planes(b, 1)
+                latent_mixed(b, 0)
+                latent_mixed(b, 1)
             if on(c):
-                project_rows(c, 0)
-                project_rows(c, 1)
-                project_columns(c, 0)
-                project_columns(c, 1)
+                project_rows(c)
+                for x in range(3):
+                    project_columns(c, x)
+                rotate(c, nc.vector if c == GROUPS - 1 else nc.gpsimd)
             if on(a):
                 quantize(a, "grp", "1")
-            if on(c):
-                rotate(c)
             if on(d):
                 store(d)

@@ -30,7 +30,7 @@ def tile_mla_pa_t_w8_kernel(tc, h_bytes, h_scale, wdq_w, wdq_s, b_dq, wuq_w, wuq
 
     with ExitStack() as ctx:
         const = ctx.enter_context(tc.tile_pool(name="const", bufs=1))
-        work = ctx.enter_context(tc.tile_pool(name="work", bufs=3))
+        work = ctx.enter_context(tc.tile_pool(name="work", bufs=4))
         psum = ctx.enter_context(tc.psum_pool(name="psum", bufs=8))
         ctx.enter_context(tc.manual_schedule())
 
@@ -72,38 +72,38 @@ def tile_mla_pa_t_w8_kernel(tc, h_bytes, h_scale, wdq_w, wdq_s, b_dq, wuq_w, wuq
         nc.scalar.activation(out=dummy2[:], in_=dummy[:], func=ACT.Sin)
         make_identity(nc, ident[:])
 
-        nc.sync.dma_start(out=hb[0][:], in_=h_view[0])
-        nc.sync.dma_start(out=wraw[:, 0:512], in_=wdq_w[0].rearrange("p n t -> p (n t)").bitcast(I32))
+        def load_group(m):
+            nc.sync.dma_start(out=hb[m][:], in_=h_view[m])
+
+        load_group(0)
         nc.sync.dma_start(out=s4[:], in_=h_scale.rearrange("o a (p t) -> p (o a t)", t=4))
+        nc.sync.dma_start(out=wraw[:, 0:512], in_=wdq_w[0].rearrange("p n t -> p (n t)").bitcast(I32))
         load_scales(wdq_s, 0, 512)
         nc.sync.dma_start(out=bdq_bf[:], in_=b_dq.rearrange("(p t) -> p t", t=4))
-        nc.sync.dma_start(out=hb[1][:], in_=h_view[1])
+        load_group(1)
+        load_group(2)
         nc.sync.dma_start(out=wraw[:, 512:896], in_=wuq_w[0].rearrange("p n t -> p (n t)").bitcast(I32))
         nc.sync.dma_start(out=wraw[:, 896:1024], in_=wqr_w[0].rearrange("p n t -> p (n t)").bitcast(I32))
+        load_group(3)
         load_scales(wuq_s, 512, 384)
         load_scales(wqr_s, 896, 128)
-        nc.sync.dma_start(out=hb[2][:], in_=h_view[2])
         nc.sync.dma_start(out=bbc[:, 0:384], in_=b_uq.partition_broadcast(P))
         nc.sync.dma_start(out=bbc[:, 384:512], in_=b_qr.partition_broadcast(P))
-        for m in range(3, GROUPS):
-            nc.sync.dma_start(out=hb[m][:], in_=h_view[m])
+        for m in range(4, GROUPS):
+            load_group(m)
 
         nc.vector.tensor_copy(out=wdq[:], in_=wraw[:, 0:512].rearrange("p (m t) -> p t m", t=4))
         nc.gpsimd.tensor_copy(out=sdq[:].rearrange("p t m -> p m t"), in_=sraw[:, 0:512].rearrange("p (m t) -> p m t", t=4))
         nc.gpsimd.tensor_copy(out=bdq[:], in_=bdq_bf[:])
 
-        def regroup(dst, src):
+        def regroup(copy, dst, src):
             uq = src[:, 0:384].rearrange("p (h c) -> p h c", c=48)
             qr = src[:, 384:512].rearrange("p (h c) -> p h c", c=16)
             for x in range(4):
-                nc.gpsimd.tensor_copy(
+                copy(
                     out=dst[:, P * x : P * (x + 1)].rearrange("p (h c) -> p h c", c=16),
                     in_=uq[:, :, 16 * x : 16 * (x + 1)] if x < 3 else qr,
                 )
-
-        regroup(wout, wraw[:, 512:1024])
-        regroup(sout, sraw[:, 512:1024])
-        regroup(bias_t, bbc)
 
         nc.gpsimd.iota(posn[:].rearrange("p (q j) -> p q j", j=4), pattern=[[512, 4], [1, 4]], base=0, channel_multiplier=4, allow_small_or_imprecise_dtypes=True)
         for i in range(4):
@@ -113,6 +113,8 @@ def tile_mla_pa_t_w8_kernel(tc, h_bytes, h_scale, wdq_w, wdq_s, b_dq, wuq_w, wuq
             nc.gpsimd.tensor_tensor(out=ang[:], in0=ang[:], in1=gem[:], op=ALU.add)
         nc.gpsimd.tensor_scalar(out=ang[:], in0=ang[:], scalar1=1.0, scalar2=-0.5, op0=ALU.mult, op1=ALU.add)
 
+        regroup(nc.gpsimd.tensor_copy, sout, sraw[:, 512:1024])
+
         def rotary_tables():
             nc.scalar.activation(out=sinw[:], in_=ang[:], func=ACT.Sin, scale=2.0 * math.pi)
             nc.scalar.activation(out=sinv[:], in_=ang[:], func=ACT.Sin, scale=math.pi)
@@ -120,7 +122,7 @@ def tile_mla_pa_t_w8_kernel(tc, h_bytes, h_scale, wdq_w, wdq_s, b_dq, wuq_w, wuq
             for half in range(2):
                 cols = slice(4 * half, 4 * half + 4)
                 nc.gpsimd.tensor_scalar(out=c8[:, :, cols], in0=sinv[:], scalar1=2.0, scalar2=-1.0, op0=ALU.mult, op1=ALU.add)
-                nc.gpsimd.tensor_scalar(out=s8[:, :, cols], in0=sinw[:], scalar1=1.0 - 2.0 * half, scalar2=0.0, op0=ALU.mult, op1=ALU.add)
+                nc.gpsimd.tensor_scalar(out=s8[:, :, cols], in0=sinw[:], scalar1=2.0 * half - 1.0, scalar2=0.0, op0=ALU.mult, op1=ALU.add)
 
         def bias_columns():
             bank = psum.tile([P, 512], F32, name="bank")
@@ -133,7 +135,7 @@ def tile_mla_pa_t_w8_kernel(tc, h_bytes, h_scale, wdq_w, wdq_s, b_dq, wuq_w, wuq
         def widen(m, b):
             s = st[m]
             if b == 0:
-                wide = work.tile([P, J * D], BF16, name="wide", align_bytes=64)
+                wide = work.tile([P, J * D], BF16, name="wide", align_bytes=64, bufs=6)
                 s["wide"] = wide
             cols = slice(1024 * b, 1024 * (b + 1))
             nc.scalar.copy(out=s["wide"][:, cols], in_=hb[m][:, cols].bitcast(F8))
@@ -206,49 +208,54 @@ def tile_mla_pa_t_w8_kernel(tc, h_bytes, h_scale, wdq_w, wdq_s, b_dq, wuq_w, wuq
 
         def interleave(m):
             s = st[m]
-            nc.vector.tensor_copy(
-                out=s["mixed"][:, 1024:2048].rearrange("p (c i t) -> p c t i", i=4, t=4),
-                in_=s["plane"][:].rearrange("p (t c i) -> p c t i", t=4, i=4),
+            nc.gpsimd.tensor_scalar(
+                out=s["mixed"][:, 1024:2048].rearrange("p (r t) -> p r t", t=4),
+                in0=s["plane"][:].rearrange("p (t r) -> p r t", t=4),
+                scalar1=1.0, scalar2=0.0, op0=ALU.mult, op1=ALU.add,
             )
 
-        def project_rows(m):
+        def rows_of(m, x, j0, j1):
+            return st[m]["rows"][:, j0:j1, :].rearrange("p j (h d) -> p j h d", d=64)[:, :, :, 16 * x : 16 * (x + 1)]
+
+        def project_rows(m, x, j0, j1):
             s = st[m]
-            rows = work.tile([P, J, 512], F32, name="rows", bufs=4)
-            s["rows"] = rows
+            chunk = slice(P * x, P * (x + 1))
             bank = psum.tile([P, 512], F32, name="bank")
-            for j in range(J):
+            for j in range(j0, j1):
                 toks = slice(P * j, P * (j + 1))
                 nc.tensor.matmul_mx(
-                    out=bank[:, P * j : P * (j + 1)], lhsT=s["c2"][:, toks].bitcast(X4), lhsT_scale=s["s2"][:, toks],
-                    rhs=wout[:, 384:512].bitcast(X4), rhs_scale=sout[:, 384:512], start=True, stop=True,
+                    out=bank[:, P * (j - j0) : P * (j - j0 + 1)], lhsT=s["c2"][:, toks].bitcast(X4), lhsT_scale=s["s2"][:, toks],
+                    rhs=wout[:, chunk].bitcast(X4), rhs_scale=sout[:, chunk], start=True, stop=True,
                 )
             nc.vector.tensor_tensor(
-                out=s["rows"][:].rearrange("p j (h d) -> p j h d", d=64)[:, :, :, 48:64],
-                in0=bank[:].rearrange("p (j h c) -> p j h c", j=J, c=16),
-                in1=bias_t[:, 384:512].rearrange("p (h c) -> p h c", c=16).unsqueeze(1).to_broadcast([P, J, HEADS, 16]),
+                out=rows_of(m, x, j0, j1),
+                in0=bank[:, 0 : P * (j1 - j0)].rearrange("p (j h c) -> p j h c", h=HEADS, c=16),
+                in1=bias_t[:, chunk].rearrange("p (h c) -> p h c", c=16).unsqueeze(1).to_broadcast([P, j1 - j0, HEADS, 16]),
                 op=ALU.add,
             )
 
-        def project_columns(m, x):
+        def project_columns(m, x, j0, j1):
             s = st[m]
-            cols = slice(P * x, P * (x + 1))
+            chunk = slice(P * x, P * (x + 1))
+            toks = slice(P * j0, P * j1)
+            width = P * (j1 - j0)
             bank = psum.tile([P, 512], F32, name="bank")
             nc.tensor.matmul_mx(
-                out=bank[:], lhsT=wout[:, cols].bitcast(X4), lhsT_scale=sout[:, cols],
-                rhs=s["c2"][:].bitcast(X4), rhs_scale=s["s2"][:], start=True, stop=True,
+                out=bank[:, 0:width], lhsT=wout[:, chunk].bitcast(X4), lhsT_scale=sout[:, chunk],
+                rhs=s["c2"][:, toks].bitcast(X4), rhs_scale=s["s2"][:, toks], start=True, stop=True,
             )
             cm = work.tile([P, 512], F32, name="cm%d" % x)
-            nc.scalar.activation(out=cm[:], in_=bank[:], func=ACT.Identity, bias=bcol[:, x : x + 1], scale=1.0)
+            nc.scalar.activation(out=cm[:, 0:width], in_=bank[:, 0:width], func=ACT.Identity, bias=bcol[:, x : x + 1], scale=1.0)
             s["cm%d" % x] = cm
 
-        def turn_back(m, x):
+        def turn_back(m, x, j0, j1):
             s = st[m]
             bank = psum.tile([P, 512], F32, name="bank")
-            for j in range(J):
+            for j in range(j1 - j0):
                 nc.tensor.transpose(bank[:, P * j : P * (j + 1)], s["cm%d" % x][:, P * j : P * (j + 1)], ident[:])
             nc.scalar.copy(
-                out=s["rows"][:].rearrange("p j (h d) -> p j h d", d=64)[:, :, :, 16 * x : 16 * (x + 1)],
-                in_=bank[:].rearrange("p (j h c) -> p j h c", j=J, c=16),
+                out=rows_of(m, x, j0, j1),
+                in_=bank[:, 0 : P * (j1 - j0)].rearrange("p (j h c) -> p j h c", h=HEADS, c=16),
             )
 
         def rotate(m, eng):
@@ -257,13 +264,13 @@ def tile_mla_pa_t_w8_kernel(tc, h_bytes, h_scale, wdq_w, wdq_s, b_dq, wuq_w, wuq
             t1 = work.tile([P, J, HEADS, 8], F32, name="t1")
             t2 = work.tile([P, J, HEADS, 8], F32, name="t2")
             eng.tensor_tensor(out=t1[:], in0=x, in1=c8[:, q : q + 4, :].unsqueeze(2).to_broadcast([P, J, HEADS, 8]), op=ALU.mult)
-            for half in range(2):
-                a = slice(4 * half, 4 * half + 4)
-                b = slice(4 - 4 * half, 8 - 4 * half)
-                eng.tensor_tensor(
-                    out=t2[:, :, :, a], in0=x[:, :, :, b], in1=s8[:, q : q + 4, a].unsqueeze(2).to_broadcast([P, J, HEADS, 4]), op=ALU.mult
-                )
-            eng.tensor_tensor(out=x, in0=t1[:], in1=t2[:], op=ALU.add)
+            eng.tensor_tensor(out=t2[:], in0=x, in1=s8[:, q : q + 4, :].unsqueeze(2).to_broadcast([P, J, HEADS, 8]), op=ALU.mult)
+            eng.tensor_tensor(
+                out=st[m]["rows"][:].rearrange("p j (h d) -> p (j h) d", d=64)[:, :, 48:56].rearrange("p g (s i) -> p g s i", s=2),
+                in0=t1[:].rearrange("p j h (s i) -> p (j h) s i", s=2),
+                in1=t2[:].rearrange("p j h (s i) -> p (j h) s i", s=2)[:, :, ::-1, :],
+                op=ALU.add,
+            )
 
         def store(m):
             nc.sync.dma_start(out=out_view[m], in_=st[m]["rows"][:].rearrange("p j f -> p (j f)"))
@@ -271,43 +278,54 @@ def tile_mla_pa_t_w8_kernel(tc, h_bytes, h_scale, wdq_w, wdq_s, b_dq, wuq_w, wuq
         def on(m):
             return 0 <= m < GROUPS
 
-        for n in range(-1, GROUPS + 3):
-            a, b, c, d, w = n, n - 1, n - 2, n - 3, n + 1
+        def by_rows(m):
+            return [(2, 0, 2), (3, 0, 4)] if m < GROUPS - 1 else [(3, 0, 4), (2, 0, 4), (1, 0, 4)]
+
+        def by_columns(m):
+            return [(0, 0, 4), (1, 0, 4), (2, 2, 4)] if m < GROUPS - 1 else [(0, 0, 4)]
+
+        for n in range(-3, GROUPS + 4):
+            a, b, c, d = n, n - 2, n - 3, n - 4
+            back = by_columns(d) if on(d) else []
+            if n == 1:
+                regroup(nc.vector.tensor_copy, wout, wraw[:, 512:1024])
+            if n == 2:
+                rotary_tables()
+                regroup(nc.scalar.copy, bias_t, bbc)
+            if n == 3:
+                bias_columns()
             if on(a):
                 turn(a, 0)
                 turn(a, 1)
-            if on(d):
-                turn_back(d, 0)
-            if on(w):
-                widen(w, 0)
-            if on(d):
-                turn_back(d, 1)
-                turn_back(d, 2)
-            if on(w):
-                widen(w, 1)
-            if n == 0:
-                rotary_tables()
-            if n == 1:
-                bias_columns()
-            if on(c):
-                interleave(c)
-            if on(a):
                 scale(a, 0)
+            if on(n + 2):
+                widen(n + 2, 1)
+            for job in back[0:1]:
+                turn_back(d, *job)
+            if on(n + 3):
+                widen(n + 3, 0)
             if on(c):
                 quantize(c, "mixed", "2")
             if on(a):
                 scale(a, 1)
+            for job in back[1:]:
+                turn_back(d, *job)
             if on(b):
                 latent_planes(b, 0)
-                latent_planes(b, 1)
                 latent_mixed(b, 0)
+            if on(n - 1):
+                quantize(n - 1, "grp", "1")
+            if on(b):
+                latent_planes(b, 1)
+                interleave(b)
                 latent_mixed(b, 1)
             if on(c):
-                project_rows(c)
-                for x in range(3):
-                    project_columns(c, x)
+                rows = work.tile([P, J, 512], F32, name="rows", bufs=6)
+                st[c]["rows"] = rows
+                for job in by_rows(c):
+                    project_rows(c, *job)
+                for job in by_columns(c):
+                    project_columns(c, *job)
                 rotate(c, nc.vector if c == GROUPS - 1 else nc.gpsimd)
-            if on(a):
-                quantize(a, "grp", "1")
             if on(d):
                 store(d)

@@ -75,7 +75,8 @@ def tile_mla_pa_t_w8_kernel(tc, h_bytes, h_scale, wdq_w, wdq_s, b_dq, wuq_w, wuq
         def load_group(m):
             nc.sync.dma_start(out=hb[m][:], in_=h_view[m])
 
-        load_group(0)
+        nc.sync.dma_start(out=hb[0][:, 0:1024], in_=h_view[0][:, 0:1024])
+        nc.sync.dma_start(out=hb[0][:, 1024:2048], in_=h_view[0][:, 1024:2048])
         nc.sync.dma_start(out=s4[:], in_=h_scale.rearrange("o a (p t) -> p (o a t)", t=4))
         nc.sync.dma_start(out=wraw[:, 0:512], in_=wdq_w[0].rearrange("p n t -> p (n t)").bitcast(I32))
         load_scales(wdq_s, 0, 512)
@@ -137,8 +138,10 @@ def tile_mla_pa_t_w8_kernel(tc, h_bytes, h_scale, wdq_w, wdq_s, b_dq, wuq_w, wuq
             if b == 0:
                 wide = work.tile([P, J * D], BF16, name="wide", align_bytes=64, bufs=6)
                 s["wide"] = wide
-            cols = slice(1024 * b, 1024 * (b + 1))
-            nc.scalar.copy(out=s["wide"][:, cols], in_=hb[m][:, cols].bitcast(F8))
+            for part in range(2 if m == 0 else 1):
+                width = 512 if m == 0 else 1024
+                cols = slice(1024 * b + width * part, 1024 * b + width * (part + 1))
+                nc.scalar.copy(out=s["wide"][:, cols], in_=hb[m][:, cols].bitcast(F8))
 
         def turn(m, b):
             bank = psum.tile([P, 512], F32, name="bank")
@@ -247,12 +250,14 @@ def tile_mla_pa_t_w8_kernel(tc, h_bytes, h_scale, wdq_w, wdq_s, b_dq, wuq_w, wuq
             cm = work.tile([P, 512], F32, name="cm%d" % x)
             nc.scalar.activation(out=cm[:, 0:width], in_=bank[:, 0:width], func=ACT.Identity, bias=bcol[:, x : x + 1], scale=1.0)
             s["cm%d" % x] = cm
+            s["first%d" % x] = j0
 
         def turn_back(m, x, j0, j1):
             s = st[m]
             bank = psum.tile([P, 512], F32, name="bank")
-            for j in range(j1 - j0):
-                nc.tensor.transpose(bank[:, P * j : P * (j + 1)], s["cm%d" % x][:, P * j : P * (j + 1)], ident[:])
+            for j in range(j0, j1):
+                src = slice(P * (j - s["first%d" % x]), P * (j - s["first%d" % x] + 1))
+                nc.tensor.transpose(bank[:, P * (j - j0) : P * (j - j0 + 1)], s["cm%d" % x][:, src], ident[:])
             nc.scalar.copy(
                 out=rows_of(m, x, j0, j1),
                 in_=bank[:, 0 : P * (j1 - j0)].rearrange("p (j h c) -> p j h c", h=HEADS, c=16),
@@ -272,21 +277,21 @@ def tile_mla_pa_t_w8_kernel(tc, h_bytes, h_scale, wdq_w, wdq_s, b_dq, wuq_w, wuq
                 op=ALU.add,
             )
 
-        def store(m):
-            nc.sync.dma_start(out=out_view[m], in_=st[m]["rows"][:].rearrange("p j f -> p (j f)"))
+        def store(m, j0, j1):
+            nc.sync.dma_start(out=out_view[m][:, 512 * j0 : 512 * j1], in_=st[m]["rows"][:, j0:j1, :].rearrange("p j f -> p (j f)"))
 
         def on(m):
             return 0 <= m < GROUPS
 
         def by_rows(m):
-            return [(2, 0, 2), (3, 0, 4)] if m < GROUPS - 1 else [(3, 0, 4), (2, 0, 4), (1, 0, 4)]
+            return [(2, 0, 2 if m % 3 and m < GROUPS - 1 else 4), (3, 0, 4)]
 
         def by_columns(m):
-            return [(0, 0, 4), (1, 0, 4), (2, 2, 4)] if m < GROUPS - 1 else [(0, 0, 4)]
+            return [(0, 0, 4), (1, 0, 4)] + ([(2, 2, 4)] if m % 3 and m < GROUPS - 1 else [])
 
         for n in range(-3, GROUPS + 4):
             a, b, c, d = n, n - 2, n - 3, n - 4
-            back = by_columns(d) if on(d) else []
+            back = by_columns(d) if on(d) and d < GROUPS - 1 else []
             if n == 1:
                 regroup(nc.vector.tensor_copy, wout, wraw[:, 512:1024])
             if n == 2:
@@ -327,5 +332,10 @@ def tile_mla_pa_t_w8_kernel(tc, h_bytes, h_scale, wdq_w, wdq_s, b_dq, wuq_w, wuq
                 for job in by_columns(c):
                     project_columns(c, *job)
                 rotate(c, nc.vector if c == GROUPS - 1 else nc.gpsimd)
-            if on(d):
-                store(d)
+            if on(d) and d < GROUPS - 1:
+                store(d, 0, J)
+            if d == GROUPS - 1:
+                for j0 in (0, 2):
+                    for x in (0, 1):
+                        turn_back(d, x, j0, j0 + 2)
+                    store(d, j0, j0 + 2)

from contextlib import ExitStack
import math

import concourse.mybir as mybir
from concourse.masks import make_identity

B, S, D, HEADS = 4, 2048, 512, 8
TOKENS = B * S
FLOPS = 2 * TOKENS * D * (D + 384 + 128)

F32 = mybir.dt.float32
BF16 = mybir.dt.bfloat16
I32 = mybir.dt.int32
U8 = mybir.dt.uint8
F8 = mybir.dt.float8_e4m3fn
X4 = mybir.dt.float8_e4m3fn_x4
ACT = mybir.ActivationFunctionType
ALU = mybir.AluOpType

P = 128
J = 4
GROUP = P * J
GROUPS = TOKENS // GROUP


def tile_mla_pa_t_w8_kernel(tc, h_bytes, h_scale, wdq_w, wdq_s, b_dq, wuq_w, wuq_s, b_uq, wqr_w, wqr_s, b_qr, out):
    nc = tc.nc
    h_view = h_bytes.rearrange("b s k -> (b s) k").rearrange("(m p j) k -> m p (j k)", p=P, j=J)
    out_view = out.rearrange("b s h d -> (b s) (h d)").rearrange("(m p j) f -> m p (j f)", p=P, j=J)

    with ExitStack() as ctx:
        const = ctx.enter_context(tc.tile_pool(name="const", bufs=1))
        work = ctx.enter_context(tc.tile_pool(name="work", bufs=4))
        psum = ctx.enter_context(tc.psum_pool(name="psum", bufs=8))
        ctx.enter_context(tc.manual_schedule())

        hb = [const.tile([P, J * D], U8, name="hb%d" % m, align_bytes=64) for m in range(GROUPS)]
        wraw = const.tile([P, 1024], I32, name="wraw", align_bytes=64)
        sraw = const.tile([P, 1024], U8, name="sraw", align_bytes=64)
        wdq = const.tile([P, 4, P], I32, name="wdq", align_bytes=64)
        sdq = const.tile([P, 4, P], U8, name="sdq", align_bytes=64)
        wout = const.tile([P, 512], I32, name="wout", align_bytes=64)
        sout = const.tile([P, 512], U8, name="sout", align_bytes=64)
        s4 = const.tile([P, 4], F32, name="s4")
        bdq_bf = const.tile([P, 4], BF16, name="bdq_bf")
        bdq = const.tile([P, 4], F32, name="bdq")
        bbc = const.tile([P, 512], BF16, name="bbc")
        bias_t = const.tile([P, 512], F32, name="bias_t")
        bcol = const.tile([P, 3], F32, name="bcol")
        ident = const.tile([P, P], F32, name="ident")
        ang = const.tile([P, 16, 4], F32, name="ang")
        gem = const.tile([P, 16, 4], F32, name="gem")
        posn = const.tile([P, 16], F32, name="posn")
        sinw = const.tile([P, 16, 4], F32, name="sinw")
        sinv = const.tile([P, 16, 4], F32, name="sinv")
        c8 = const.tile([P, 16, 8], F32, name="c8")
        s8 = const.tile([P, 16, 8], F32, name="s8")
        dummy = const.tile([P, 1], F32, name="dummy")
        dummy2 = const.tile([P, 1], F32, name="dummy2")

        sraw32 = sraw[:].bitcast(I32)

        def load_scales(src, first, width):
            for q in range(4):
                nc.sync.dma_start(
                    out=sraw32[32 * q : 32 * q + 4, first // 4 : (first + width) // 4],
                    in_=src[0][4 * q : 4 * q + 4, :].bitcast(I32),
                )

        nc.vector.memset(sraw32, 0)
        nc.vector.memset(dummy[:], 0.0)
        nc.scalar.activation(out=dummy2[:], in_=dummy[:], func=ACT.Sin)
        make_identity(nc, ident[:])

        def load_group(m):
            nc.sync.dma_start(out=hb[m][:], in_=h_view[m])

        nc.sync.dma_start(out=hb[0][:, 0:1024], in_=h_view[0][:, 0:1024])
        nc.sync.dma_start(out=hb[0][:, 1024:2048], in_=h_view[0][:, 1024:2048])
        nc.sync.dma_start(out=s4[:], in_=h_scale.rearrange("o a (p t) -> p (o a t)", t=4))
        nc.sync.dma_start(out=wraw[:, 0:512], in_=wdq_w[0].rearrange("p n t -> p (n t)").bitcast(I32))
        load_scales(wdq_s, 0, 512)
        nc.sync.dma_start(out=bdq_bf[:], in_=b_dq.rearrange("(p t) -> p t", t=4))
        load_group(1)
        load_group(2)
        nc.sync.dma_start(out=wraw[:, 512:896], in_=wuq_w[0].rearrange("p n t -> p (n t)").bitcast(I32))
        nc.sync.dma_start(out=wraw[:, 896:1024], in_=wqr_w[0].rearrange("p n t -> p (n t)").bitcast(I32))
        load_group(3)
        load_scales(wuq_s, 512, 384)
        load_scales(wqr_s, 896, 128)
        nc.sync.dma_start(out=bbc[:, 0:384], in_=b_uq.partition_broadcast(P))
        nc.sync.dma_start(out=bbc[:, 384:512], in_=b_qr.partition_broadcast(P))
        for m in range(4, GROUPS):
            load_group(m)

        nc.vector.tensor_copy(out=wdq[:], in_=wraw[:, 0:512].rearrange("p (m t) -> p t m", t=4))
        nc.gpsimd.tensor_copy(out=sdq[:].rearrange("p t m -> p m t"), in_=sraw[:, 0:512].rearrange("p (m t) -> p m t", t=4))
        nc.gpsimd.tensor_copy(out=bdq[:], in_=bdq_bf[:])

        def regroup(copy, dst, src):
            uq = src[:, 0:384].rearrange("p (h c) -> p h c", c=48)
            qr = src[:, 384:512].rearrange("p (h c) -> p h c", c=16)
            for x in range(4):
                copy(
                    out=dst[:, P * x : P * (x + 1)].rearrange("p (h c) -> p h c", c=16),
                    in_=uq[:, :, 16 * x : 16 * (x + 1)] if x < 3 else qr,
                )

        nc.gpsimd.iota(posn[:].rearrange("p (q j) -> p q j", j=4), pattern=[[512, 4], [1, 4]], base=0, channel_multiplier=4, allow_small_or_imprecise_dtypes=True)
        for i in range(4):
            nc.gpsimd.tensor_scalar(out=ang[:, :, i], in0=posn[:], scalar1=1.0 / (80.0 * math.pi * 10.0**i), scalar2=None, op0=ALU.mult)
        for turns in (8.0, 4.0, 2.0, 1.0):
            nc.gpsimd.tensor_scalar(out=gem[:], in0=ang[:], scalar1=turns, scalar2=-turns, op0=ALU.is_ge, op1=ALU.mult)
            nc.gpsimd.tensor_tensor(out=ang[:], in0=ang[:], in1=gem[:], op=ALU.add)
        nc.gpsimd.tensor_scalar(out=ang[:], in0=ang[:], scalar1=1.0, scalar2=-0.5, op0=ALU.mult, op1=ALU.add)

        regroup(nc.gpsimd.tensor_copy, sout, sraw[:, 512:1024])

        def rotary_tables():
            nc.scalar.activation(out=sinw[:], in_=ang[:], func=ACT.Sin, scale=2.0 * math.pi)
            nc.scalar.activation(out=sinv[:], in_=ang[:], func=ACT.Sin, scale=math.pi)
            nc.gpsimd.tensor_tensor(out=sinv[:], in0=sinv[:], in1=sinv[:], op=ALU.mult)
            for half in range(2):
                cols = slice(4 * half, 4 * half + 4)
                nc.gpsimd.tensor_scalar(out=c8[:, :, cols], in0=sinv[:], scalar1=2.0, scalar2=-1.0, op0=ALU.mult, op1=ALU.add)
                nc.gpsimd.tensor_scalar(out=s8[:, :, cols], in0=sinw[:], scalar1=2.0 * half - 1.0, scalar2=0.0, op0=ALU.mult, op1=ALU.add)

        def bias_columns():
            bank = psum.tile([P, 512], F32, name="bank")
            for x in range(3):
                nc.tensor.transpose(bank[:, P * x : P * (x + 1)], bias_t[:, P * x : P * (x + 1)], ident[:])
            nc.vector.tensor_copy(out=bcol[:], in_=bank[:, 0:384].rearrange("p (x r) -> p x r", x=3)[:, :, 0])

        st = [{} for m in range(GROUPS)]

        def widen(m, b):
            s = st[m]
            if b == 0:
                wide = work.tile([P, J * D], BF16, name="wide", align_bytes=64, bufs=6)
                s["wide"] = wide
            for part in range(2 if m == 0 else 1):
                width = 512 if m == 0 else 1024
                cols = slice(1024 * b + width * part, 1024 * b + width * (part + 1))
                nc.scalar.copy(out=s["wide"][:, cols], in_=hb[m][:, cols].bitcast(F8))

        def turn(m, b):
            bank = psum.tile([P, 512], F32, name="bank")
            view = bank[:].rearrange("p (u r) -> p u r", u=2)
            words = st[m]["wide"][:].bitcast(F32)
            for jj in range(2):
                for u in range(2):
                    base = 256 * (2 * b + jj)
                    nc.tensor.transpose(view[:, u, P * jj : P * (jj + 1)], words[:, base + u : base + 256 : 2], ident[:])
            st[m]["x%d" % b] = bank

        def scale(m, b):
            s = st[m]
            if b == 0:
                grp = work.tile([P, J * D], BF16, name="grp", align_bytes=64)
                s["grp"] = grp
            nc.vector.tensor_tensor(
                out=s["grp"][:, 1024 * b : 1024 * (b + 1)].rearrange("p (r u e) -> p r u e", u=2, e=2),
                in0=s["x%d" % b][:].bitcast(BF16).rearrange("p (u r e) -> p r u e", u=2, e=2),
                in1=s4[:].rearrange("p (u e) -> p u e", u=2).unsqueeze(1).to_broadcast([P, 256, 2, 2]),
                op=ALU.mult,
            )

        def quantize(m, src, tag):
            codes = work.tile([P, 512], I32, name="codes" + tag, align_bytes=64)
            scales = work.tile([P, 512], U8, name="scales" + tag, align_bytes=64)
            nc.vector.quantize_mx(out=codes[:].bitcast(X4), scales=scales[:], in_=st[m][src][:])
            st[m]["c" + tag] = codes
            st[m]["s" + tag] = scales

        def latent_mm(m, out, t, toks):
            s = st[m]
            nc.tensor.matmul_mx(
                out=out, lhsT=wdq[:, t, :].bitcast(X4), lhsT_scale=sdq[:, t, :],
                rhs=s["c1"][:, toks].bitcast(X4), rhs_scale=s["s1"][:, toks], start=True, stop=True,
            )

        def latent_planes(m, half):
            s = st[m]
            bank = psum.tile([P, 512], F32, name="bank")
            if half == 0:
                plane = work.tile([P, 1024], BF16, name="plane", align_bytes=64)
                s["plane"] = plane
            for i in range(2):
                t = 2 * half + i
                latent_mm(m, bank[:, 256 * i : 256 * (i + 1)], t, slice(256, 512))
            for i in range(2):
                t = 2 * half + i
                nc.scalar.activation(
                    out=s["plane"][:, 256 * t : 256 * (t + 1)], in_=bank[:, 256 * i : 256 * (i + 1)], func=ACT.Identity, bias=bdq[:, t : t + 1], scale=1.0
                )

        def latent_mixed(m, j):
            s = st[m]
            bank = psum.tile([P, 512], F32, name="bank")
            if j == 0:
                mixed = work.tile([P, J * D], BF16, name="mixed", align_bytes=64)
                s["mixed"] = mixed
            for t in range(4):
                latent_mm(m, bank[:, P * t : P * (t + 1)], t, slice(P * j, P * (j + 1)))
            nc.vector.tensor_tensor(
                out=s["mixed"][:, 512 * j : 512 * (j + 1)].rearrange("p (r t) -> p r t", t=4),
                in0=bank[:].rearrange("p (t r) -> p r t", t=4),
                in1=bdq[:].unsqueeze(1).to_broadcast([P, P, 4]),
                op=ALU.add,
            )

        def interleave(m):
            s = st[m]
            nc.gpsimd.tensor_scalar(
                out=s["mixed"][:, 1024:2048].rearrange("p (r t) -> p r t", t=4),
                in0=s["plane"][:].rearrange("p (t r) -> p r t", t=4),
                scalar1=1.0, scalar2=0.0, op0=ALU.mult, op1=ALU.add,
            )

        def rows_of(m, x, j0, j1):
            return st[m]["rows"][:, j0:j1, :].rearrange("p j (h d) -> p j h d", d=64)[:, :, :, 16 * x : 16 * (x + 1)]

        def project_rows(m, x, j0, j1):
            s = st[m]
            chunk = slice(P * x, P * (x + 1))
            bank = psum.tile([P, 512], F32, name="bank")
            for j in range(j0, j1):
                toks = slice(P * j, P * (j + 1))
                nc.tensor.matmul_mx(
                    out=bank[:, P * (j - j0) : P * (j - j0 + 1)], lhsT=s["c2"][:, toks].bitcast(X4), lhsT_scale=s["s2"][:, toks],
                    rhs=wout[:, chunk].bitcast(X4), rhs_scale=sout[:, chunk], start=True, stop=True,
                )
            nc.vector.tensor_tensor(
                out=rows_of(m, x, j0, j1),
                in0=bank[:, 0 : P * (j1 - j0)].rearrange("p (j h c) -> p j h c", h=HEADS, c=16),
                in1=bias_t[:, chunk].rearrange("p (h c) -> p h c", c=16).unsqueeze(1).to_broadcast([P, j1 - j0, HEADS, 16]),
                op=ALU.add,
            )

        def project_columns(m, x, j0, j1):
            s = st[m]
            chunk = slice(P * x, P * (x + 1))
            toks = slice(P * j0, P * j1)
            width = P * (j1 - j0)
            bank = psum.tile([P, 512], F32, name="bank")
            nc.tensor.matmul_mx(
                out=bank[:, 0:width], lhsT=wout[:, chunk].bitcast(X4), lhsT_scale=sout[:, chunk],
                rhs=s["c2"][:, toks].bitcast(X4), rhs_scale=s["s2"][:, toks], start=True, stop=True,
            )
            cm = work.tile([P, 512], F32, name="cm%d" % x)
            nc.scalar.activation(out=cm[:, 0:width], in_=bank[:, 0:width], func=ACT.Identity, bias=bcol[:, x : x + 1], scale=1.0)
            s["cm%d" % x] = cm
            s["first%d" % x] = j0

        def turn_back(m, x, j0, j1):
            s = st[m]
            bank = psum.tile([P, 512], F32, name="bank")
            for j in range(j0, j1):
                src = slice(P * (j - s["first%d" % x]), P * (j - s["first%d" % x] + 1))
                nc.tensor.transpose(bank[:, P * (j - j0) : P * (j - j0 + 1)], s["cm%d" % x][:, src], ident[:])
            nc.scalar.copy(
                out=rows_of(m, x, j0, j1),
                in_=bank[:, 0 : P * (j1 - j0)].rearrange("p (j h c) -> p j h c", h=HEADS, c=16),
            )

        def rotate(m, eng):
            x = st[m]["rows"][:].rearrange("p j (h d) -> p j h d", d=64)[:, :, :, 48:56]
            q = 4 * (m % 4)
            t1 = work.tile([P, J, HEADS, 8], F32, name="t1")
            t2 = work.tile([P, J, HEADS, 8], F32, name="t2")
            eng.tensor_tensor(out=t1[:], in0=x, in1=c8[:, q : q + 4, :].unsqueeze(2).to_broadcast([P, J, HEADS, 8]), op=ALU.mult)
            eng.tensor_tensor(out=t2[:], in0=x, in1=s8[:, q : q + 4, :].unsqueeze(2).to_broadcast([P, J, HEADS, 8]), op=ALU.mult)
            eng.tensor_tensor(
                out=st[m]["rows"][:].rearrange("p j (h d) -> p (j h) d", d=64)[:, :, 48:56].rearrange("p g (s i) -> p g s i", s=2),
                in0=t1[:].rearrange("p j h (s i) -> p (j h) s i", s=2),
                in1=t2[:].rearrange("p j h (s i) -> p (j h) s i", s=2)[:, :, ::-1, :],
                op=ALU.add,
            )

        def store(m, j0, j1):
            nc.sync.dma_start(out=out_view[m][:, 512 * j0 : 512 * j1], in_=st[m]["rows"][:, j0:j1, :].rearrange("p j f -> p (j f)"))

        def on(m):
            return 0 <= m < GROUPS

        def by_rows(m):
            return [(2, 0, 2 if m % 3 and m < GROUPS - 1 else 4), (3, 0, 4)]

        def by_columns(m):
            return [(0, 0, 4), (1, 0, 4)] + ([(2, 2, 4)] if m % 3 and m < GROUPS - 1 else [])

        for n in range(-3, GROUPS + 4):
            a, b, c, d = n, n - 2, n - 3, n - 4
            back = by_columns(d) if on(d) and d < GROUPS - 1 else []
            if n == 1:
                regroup(nc.vector.tensor_copy, wout, wraw[:, 512:1024])
            if n == 2:
                rotary_tables()
                regroup(nc.scalar.copy, bias_t, bbc)
            if n == 3:
                bias_columns()
            if on(a):
                turn(a, 0)
                turn(a, 1)
                scale(a, 0)
            if on(n + 2):
                widen(n + 2, 1)
            for job in back[0:1]:
                turn_back(d, *job)
            if on(n + 3):
                widen(n + 3, 0)
            if on(c):
                quantize(c, "mixed", "2")
            if on(a):
                scale(a, 1)
            for job in back[1:]:
                turn_back(d, *job)
            if on(b):
                latent_planes(b, 0)
                latent_mixed(b, 0)
            if on(n - 1):
                quantize(n - 1, "grp", "1")
            if on(b):
                latent_planes(b, 1)
                interleave(b)
                latent_mixed(b, 1)
            if on(c):
                rows = work.tile([P, J, 512], F32, name="rows", bufs=6)
                st[c]["rows"] = rows
                for job in by_rows(c):
                    project_rows(c, *job)
                for job in by_columns(c):
                    project_columns(c, *job)
                rotate(c, nc.vector if c == GROUPS - 1 else nc.gpsimd)
            if on(d) and d < GROUPS - 1:
                store(d, 0, J)
            if d == GROUPS - 1:
                for j0 in (0, 2):
                    for x in (0, 1):
                        turn_back(d, x, j0, j0 + 2)
                    store(d, j0, j0 + 2)
